import numpy as np
import ml_dtypes


def mxq(x, axis, fmt="e4m3"):
    dtype, down = {"e4m3": (ml_dtypes.float8_e4m3fn, 7), "e5m2": (ml_dtypes.float8_e5m2, 14)}[fmt]
    v = np.moveaxis(np.asarray(x, np.float32).astype(ml_dtypes.bfloat16).astype(np.float64), axis, -1)
    blocks = v.reshape(v.shape[:-1] + (-1, 32))
    amax = np.abs(blocks).max(-1, keepdims=True)
    byte = np.maximum(np.where(amax > 0, np.frexp(amax)[1] - 1 + 127, 0) - down, 1)
    scale = np.exp2(byte - 127.0)
    codes = (blocks / scale).astype(np.float32).astype(dtype).astype(np.float64)
    return np.moveaxis((codes * scale).reshape(v.shape), -1, axis)


WIDE = False


def mx_kscale(k):
    if not WIDE:
        return np.ones(k)
    levels = np.array([20, -20, 10, -10, 0])
    a = np.random.permutation(np.resize(levels, k // 512 * 4)).reshape(k // 512, 4)
    idx = np.arange(k)
    return np.exp2(a[idx // 512, idx % 128 // 32])


BF16 = ml_dtypes.bfloat16


def bf(x):
    return np.asarray(x, np.float32).astype(BF16)


def f64(x):
    return np.asarray(x).astype(np.float64)


B, S, DIN, DOUT = 2, 512, 2048, 2048
T = B * S
BLK = 32


def grid_draw(shape, n):
    v = np.random.randint(-127, 128, shape + (n,))
    pos = np.random.randint(0, n, shape + (1,))
    sgn = 2 * np.random.randint(0, 2, shape + (1,)) - 1
    np.put_along_axis(v, pos, 127 * sgn, axis=-1)
    return v


def setup_inputs():
    s = mx_kscale(T).reshape(B, S, 1)
    x = grid_draw((B, S, DIN // BLK), BLK).reshape(B, S, DIN) / 64.0 * s
    w = grid_draw((DOUT // BLK, DIN // BLK), BLK * BLK).reshape(DOUT // BLK, DIN // BLK, BLK, BLK)
    w = w.transpose(0, 2, 1, 3).reshape(DOUT, DIN) / 4096.0
    b = np.random.standard_normal(DOUT) * 0.5
    g = np.random.standard_normal((B, S, DOUT)) * np.exp2(np.random.randint(-12, 1, (B, S, 1))) / s
    return {"x": bf(x), "weight": bf(w), "bias": bf(b), "grad_out": bf(g)}


def reference(x, weight, bias, grad_out):
    x2 = f64(x).reshape(T, DIN)
    g2 = f64(grad_out).reshape(T, DOUT)
    return mxq(g2, 0, "e5m2").T @ mxq(x2, 0, "e4m3")

@@ -1,0 +1,107 @@
+from contextlib import ExitStack
+
+import concourse.mybir as mybir
+
+BF16 = mybir.dt.bfloat16
+F32 = mybir.dt.float32
+U32 = mybir.dt.uint32
+U8 = mybir.dt.uint8
+E4M3_X4 = mybir.dt.float8_e4m3fn_x4
+E5M2_X4 = mybir.dt.float8_e5m2_x4
+
+P = 128
+PACK = 4
+PASSES = 2
+DIN = 2048
+DOUT = 2048
+M_TILE = 128
+N_TILE = 512
+PIECE = 512
+M_TILES_PER_PIECE = PIECE // M_TILE
+N_TILES = DIN // N_TILE
+G_PIECES = DOUT // PIECE
+X_PIECES = DIN // PIECE
+
+FLOPS = 2 * PASSES * P * PACK * DIN * DOUT
+BYTES = 2 * PASSES * P * PACK * (DIN + DOUT) + 4 * DIN * DOUT
+
+
+def tile_linearmem_kernel(tc, x, weight, bias, grad_out, out):
+    nc = tc.nc
+    x_rows = x.rearrange("b (p j) d -> b p j d", j=PACK)
+    g_rows = grad_out.rearrange("b (p j) e -> b p j e", j=PACK)
+
+    with ExitStack() as ctx:
+        raw = ctx.enter_context(tc.tile_pool(name="raw", bufs=1))
+        keep = ctx.enter_context(tc.tile_pool(name="keep", bufs=1))
+        stage = ctx.enter_context(tc.tile_pool(name="stage", bufs=4))
+        result = ctx.enter_context(tc.tile_pool(name="result", bufs=8))
+        psum = ctx.enter_context(tc.psum_pool(name="psum", bufs=8))
+
+        x_raw = [raw.tile([P, PACK, DIN], BF16, name="x_raw%d" % c) for c in range(PASSES)]
+        g_raw = [raw.tile([P, PACK, DOUT], BF16, name="g_raw%d" % c) for c in range(PASSES)]
+        for c in range(PASSES):
+            nc.sync.dma_start(out=g_raw[c][:, :, 0:PIECE], in_=g_rows[c][:, :, 0:PIECE])
+        for c in range(PASSES):
+            nc.sync.dma_start(out=x_raw[c][:], in_=x_rows[c])
+        for c in range(PASSES):
+            nc.sync.dma_start(out=g_raw[c][:, :, PIECE:DOUT], in_=g_rows[c][:, :, PIECE:DOUT])
+
+        x_codes = keep.tile([P, PASSES, DIN], U32, align_bytes=64)
+        x_scales = keep.tile([P, PASSES, DIN], U8, align_bytes=64)
+        g_codes = keep.tile([P, PASSES, DOUT], U32, align_bytes=64)
+        g_scales = keep.tile([P, PASSES, DOUT], U8, align_bytes=64)
+
+        def quantise_piece(copy, rows, codes, scales, packed_dtype):
+            grouped = stage.tile([P, PIECE, PACK], BF16, align_bytes=64)
+            copy(
+                out=grouped[:].rearrange("p (w i) j -> p w j i", i=4),
+                in_=rows.rearrange("p j (w i) -> p w j i", i=4),
+            )
+            nc.vector.quantize_mx(
+                out=codes.bitcast(packed_dtype),
+                scales=scales,
+                in_=grouped[:].rearrange("p w j -> p (w j)"),
+            )
+
+        def quantise_g(copy, piece, c):
+            cols = slice(piece * PIECE, (piece + 1) * PIECE)
+            quantise_piece(copy, g_raw[c][:, :, cols], g_codes[:, c, cols], g_scales[:, c, cols], E5M2_X4)
+
+        def quantise_x(copy, piece, c):
+            cols = slice(piece * PIECE, (piece + 1) * PIECE)
+            quantise_piece(copy, x_raw[c][:, :, cols], x_codes[:, c, cols], x_scales[:, c, cols], E4M3_X4)
+
+        for c in range(PASSES):
+            quantise_g((nc.vector.tensor_copy, nc.scalar.copy)[c % 2], 0, c)
+        for c in range(PASSES):
+            for piece in range(X_PIECES):
+                quantise_x((nc.vector.tensor_copy, nc.scalar.copy)[piece % 2], piece, c)
+
+        for piece in range(G_PIECES):
+            if piece + 1 < G_PIECES:
+                for c in range(PASSES):
+                    quantise_g(nc.vector.tensor_copy, piece + 1, c)
+            for m in range(piece * M_TILES_PER_PIECE, (piece + 1) * M_TILES_PER_PIECE):
+                m_cols = slice(m * M_TILE, (m + 1) * M_TILE)
+                banks = [psum.tile([P, N_TILE], F32, name="bank") for n in range(N_TILES)]
+                for c in range(PASSES):
+                    for n in range(N_TILES):
+                        n_cols = slice(n * N_TILE, (n + 1) * N_TILE)
+                        nc.tensor.matmul_mx(
+                            out=banks[n][:],
+                            lhsT=g_codes[:, c, m_cols].bitcast(E5M2_X4),
+                            lhsT_scale=g_scales[:, c, m_cols],
+                            rhs=x_codes[:, c, n_cols].bitcast(E4M3_X4),
+                            rhs_scale=x_scales[:, c, n_cols],
+                            start=(c == 0),
+                            stop=(c == PASSES - 1),
+                        )
+                out_rows = result.tile([P, DIN], F32)
+                for n in range(N_TILES):
+                    n_cols = slice(n * N_TILE, (n + 1) * N_TILE)
+                    if n == N_TILES - 1:
+                        nc.vector.tensor_copy(out=out_rows[:, n_cols], in_=banks[n][:])
+                    else:
+                        nc.scalar.copy(out=out_rows[:, n_cols], in_=banks[n][:])
+                nc.sync.dma_start(out=out[m_cols, :], in_=out_rows[:])

@@ -39,13 +39,14 @@ def tile_linearmem_kernel(tc, x, weight, bias, grad_out, out):
         psum = ctx.enter_context(tc.psum_pool(name="psum", bufs=8))
 
         x_raw = [raw.tile([P, PACK, DIN], BF16, name="x_raw%d" % c) for c in range(PASSES)]
-        g_raw = [raw.tile([P, PACK, DOUT], BF16, name="g_raw%d" % c) for c in range(PASSES)]
+        g_first = [raw.tile([P, PACK, PIECE], BF16, name="g_first%d" % c) for c in range(PASSES)]
+        g_rest = [raw.tile([P, PACK, DOUT - PIECE], BF16, name="g_rest%d" % c) for c in range(PASSES)]
         for c in range(PASSES):
-            nc.sync.dma_start(out=g_raw[c][:, :, 0:PIECE], in_=g_rows[c][:, :, 0:PIECE])
+            nc.sync.dma_start(out=g_first[c][:], in_=g_rows[c][:, :, 0:PIECE])
         for c in range(PASSES):
             nc.sync.dma_start(out=x_raw[c][:], in_=x_rows[c])
         for c in range(PASSES):
-            nc.sync.dma_start(out=g_raw[c][:, :, PIECE:DOUT], in_=g_rows[c][:, :, PIECE:DOUT])
+            nc.sync.dma_start(out=g_rest[c][:], in_=g_rows[c][:, :, PIECE:DOUT])
 
         x_codes = keep.tile([P, PASSES, DIN], U32, align_bytes=64)
         x_scales = keep.tile([P, PASSES, DIN], U8, align_bytes=64)
@@ -66,7 +67,8 @@ def tile_linearmem_kernel(tc, x, weight, bias, grad_out, out):
 
         def quantise_g(copy, piece, c):
             cols = slice(piece * PIECE, (piece + 1) * PIECE)
-            quantise_piece(copy, g_raw[c][:, :, cols], g_codes[:, c, cols], g_scales[:, c, cols], E5M2_X4)
+            rows = g_first[c][:] if piece == 0 else g_rest[c][:, :, (piece - 1) * PIECE : piece * PIECE]
+            quantise_piece(copy, rows, g_codes[:, c, cols], g_scales[:, c, cols], E5M2_X4)
 
         def quantise_x(copy, piece, c):
             cols = slice(piece * PIECE, (piece + 1) * PIECE)

@@ -16,9 +16,12 @@ DIN = 2048
 DOUT = 2048
 M_TILE = 128
 N_TILE = 512
+M_TILES = DOUT // M_TILE
+N_TILES = DIN // N_TILE
+PSUM_BANKS = 8
+EARLY = PSUM_BANKS // N_TILES
 PIECE = 512
 M_TILES_PER_PIECE = PIECE // M_TILE
-N_TILES = DIN // N_TILE
 G_PIECES = DOUT // PIECE
 X_PIECES = DIN // PIECE
 
@@ -34,9 +37,10 @@ def tile_linearmem_kernel(tc, x, weight, bias, grad_out, out):
     with ExitStack() as ctx:
         raw = ctx.enter_context(tc.tile_pool(name="raw", bufs=1))
         keep = ctx.enter_context(tc.tile_pool(name="keep", bufs=1))
-        stage = ctx.enter_context(tc.tile_pool(name="stage", bufs=4))
+        stage = ctx.enter_context(tc.tile_pool(name="stage", bufs=6))
         result = ctx.enter_context(tc.tile_pool(name="result", bufs=8))
-        psum = ctx.enter_context(tc.psum_pool(name="psum", bufs=8))
+        psum = ctx.enter_context(tc.psum_pool(name="psum", bufs=PSUM_BANKS))
+        ctx.enter_context(tc.manual_schedule())
 
         x_raw = [raw.tile([P, PACK, DIN], BF16, name="x_raw%d" % c) for c in range(PASSES)]
         g_first = [raw.tile([P, PACK, PIECE], BF16, name="g_first%d" % c) for c in range(PASSES)]
@@ -53,57 +57,71 @@ def tile_linearmem_kernel(tc, x, weight, bias, grad_out, out):
         g_codes = keep.tile([P, PASSES, DOUT], U32, align_bytes=64)
         g_scales = keep.tile([P, PASSES, DOUT], U8, align_bytes=64)
 
-        def quantise_piece(copy, rows, codes, scales, packed_dtype):
-            grouped = stage.tile([P, PIECE, PACK], BF16, align_bytes=64)
+        def regroup(copy, rows):
+            grouped = stage.tile([P, PIECE, PACK], BF16, align_bytes=64, name="grouped")
             copy(
-                out=grouped[:].rearrange("p (w i) j -> p w j i", i=4),
-                in_=rows.rearrange("p j (w i) -> p w j i", i=4),
+                out=grouped[:].rearrange("p (v i) j -> p v j i", i=4),
+                in_=rows.rearrange("p j (v i) -> p v j i", i=4),
             )
+            return grouped
+
+        def quantise(grouped, codes, scales, piece, c, packed_dtype):
+            cols = slice(piece * PIECE, (piece + 1) * PIECE)
             nc.vector.quantize_mx(
-                out=codes.bitcast(packed_dtype),
-                scales=scales,
-                in_=grouped[:].rearrange("p w j -> p (w j)"),
+                out=codes[:, c, cols].bitcast(packed_dtype),
+                scales=scales[:, c, cols],
+                in_=grouped[:].rearrange("p v j -> p (v j)"),
             )
 
-        def quantise_g(copy, piece, c):
-            cols = slice(piece * PIECE, (piece + 1) * PIECE)
-            rows = g_first[c][:] if piece == 0 else g_rest[c][:, :, (piece - 1) * PIECE : piece * PIECE]
-            quantise_piece(copy, rows, g_codes[:, c, cols], g_scales[:, c, cols], E5M2_X4)
+        def g_piece_rows(piece, c):
+            return g_first[c][:] if piece == 0 else g_rest[c][:, :, (piece - 1) * PIECE : piece * PIECE]
 
-        def quantise_x(copy, piece, c):
-            cols = slice(piece * PIECE, (piece + 1) * PIECE)
-            quantise_piece(copy, x_raw[c][:, :, cols], x_codes[:, c, cols], x_scales[:, c, cols], E4M3_X4)
+        def multiply(banks, m, n, c):
+            nc.tensor.matmul_mx(
+                out=banks[n][:],
+                lhsT=g_codes[:, c, m * M_TILE : (m + 1) * M_TILE].bitcast(E5M2_X4),
+                lhsT_scale=g_scales[:, c, m * M_TILE : (m + 1) * M_TILE],
+                rhs=x_codes[:, c, n * N_TILE : (n + 1) * N_TILE].bitcast(E4M3_X4),
+                rhs_scale=x_scales[:, c, n * N_TILE : (n + 1) * N_TILE],
+                start=(c == 0),
+                stop=(c == PASSES - 1),
+            )
 
+        def open_banks():
+            return [psum.tile([P, N_TILE], F32, name="bank") for n in range(N_TILES)]
+
+        def finish(banks, m):
+            out_rows = result.tile([P, DIN], F32, name="out_rows")
+            for n in range(N_TILES):
+                copy = nc.vector.tensor_copy if n == N_TILES - 1 else nc.scalar.copy
+                copy(out=out_rows[:, n * N_TILE : (n + 1) * N_TILE], in_=banks[n][:])
+            nc.sync.dma_start(out=out[m * M_TILE : (m + 1) * M_TILE, :], in_=out_rows[:])
+            piece, c = m // M_TILES_PER_PIECE + 1, m % M_TILES_PER_PIECE - 1
+            if piece < G_PIECES and c in range(PASSES):
+                quantise(regroup(nc.vector.tensor_copy, g_piece_rows(piece, c)), g_codes, g_scales, piece, c, E5M2_X4)
+
+        copies = (nc.vector.tensor_copy, nc.scalar.copy)
+        g_grouped = [regroup(copies[c], g_piece_rows(0, c)) for c in range(PASSES)]
         for c in range(PASSES):
-            quantise_g((nc.vector.tensor_copy, nc.scalar.copy)[c % 2], 0, c)
+            quantise(g_grouped[c], g_codes, g_scales, 0, c, E5M2_X4)
+
+        early_banks = [open_banks() for m in range(EARLY)]
         for c in range(PASSES):
+            x_grouped = [
+                regroup(copies[piece % 2], x_raw[c][:, :, piece * PIECE : (piece + 1) * PIECE])
+                for piece in range(X_PIECES)
+            ]
             for piece in range(X_PIECES):
-                quantise_x((nc.vector.tensor_copy, nc.scalar.copy)[piece % 2], piece, c)
+                quantise(x_grouped[piece], x_codes, x_scales, piece, c, E4M3_X4)
+            for n in range(N_TILES):
+                for m in range(EARLY):
+                    multiply(early_banks[m], m, n, c)
+        for m in range(EARLY):
+            finish(early_banks[m], m)
 
-        for piece in range(G_PIECES):
-            if piece + 1 < G_PIECES:
-                for c in range(PASSES):
-                    quantise_g(nc.vector.tensor_copy, piece + 1, c)
-            for m in range(piece * M_TILES_PER_PIECE, (piece + 1) * M_TILES_PER_PIECE):
-                m_cols = slice(m * M_TILE, (m + 1) * M_TILE)
-                banks = [psum.tile([P, N_TILE], F32, name="bank") for n in range(N_TILES)]
-                for c in range(PASSES):
-                    for n in range(N_TILES):
-                        n_cols = slice(n * N_TILE, (n + 1) * N_TILE)
-                        nc.tensor.matmul_mx(
-                            out=banks[n][:],
-                            lhsT=g_codes[:, c, m_cols].bitcast(E5M2_X4),
-                            lhsT_scale=g_scales[:, c, m_cols],
-                            rhs=x_codes[:, c, n_cols].bitcast(E4M3_X4),
-                            rhs_scale=x_scales[:, c, n_cols],
-                            start=(c == 0),
-                            stop=(c == PASSES - 1),
-                        )
-                out_rows = result.tile([P, DIN], F32)
+        for m in range(EARLY, M_TILES):
+            banks = open_banks()
+            for c in range(PASSES):
                 for n in range(N_TILES):
-                    n_cols = slice(n * N_TILE, (n + 1) * N_TILE)
-                    if n == N_TILES - 1:
-                        nc.vector.tensor_copy(out=out_rows[:, n_cols], in_=banks[n][:])
-                    else:
-                        nc.scalar.copy(out=out_rows[:, n_cols], in_=banks[n][:])
-                nc.sync.dma_start(out=out[m_cols, :], in_=out_rows[:])
+                    multiply(banks, m, n, c)
+            finish(banks, m)

@@ -24,6 +24,8 @@ PIECE = 512
 M_TILES_PER_PIECE = PIECE // M_TILE
 G_PIECES = DOUT // PIECE
 X_PIECES = DIN // PIECE
+X_CUTS = 2
+X_PIECES_PER_CUT = X_PIECES // X_CUTS
 
 FLOPS = 2 * PASSES * P * PACK * DIN * DOUT
 BYTES = 2 * PASSES * P * PACK * (DIN + DOUT) + 4 * DIN * DOUT
@@ -42,13 +44,18 @@ def tile_linearmem_kernel(tc, x, weight, bias, grad_out, out):
         psum = ctx.enter_context(tc.psum_pool(name="psum", bufs=PSUM_BANKS))
         ctx.enter_context(tc.manual_schedule())
 
-        x_raw = [raw.tile([P, PACK, DIN], BF16, name="x_raw%d" % c) for c in range(PASSES)]
+        x_raw = [
+            [raw.tile([P, PACK, DIN // X_CUTS], BF16, name="x_raw%d_%d" % (c, cut)) for cut in range(X_CUTS)]
+            for c in range(PASSES)
+        ]
         g_first = [raw.tile([P, PACK, PIECE], BF16, name="g_first%d" % c) for c in range(PASSES)]
         g_rest = [raw.tile([P, PACK, DOUT - PIECE], BF16, name="g_rest%d" % c) for c in range(PASSES)]
         for c in range(PASSES):
             nc.sync.dma_start(out=g_first[c][:], in_=g_rows[c][:, :, 0:PIECE])
         for c in range(PASSES):
-            nc.sync.dma_start(out=x_raw[c][:], in_=x_rows[c])
+            for cut in range(X_CUTS):
+                cut_cols = slice(cut * (DIN // X_CUTS), (cut + 1) * (DIN // X_CUTS))
+                nc.sync.dma_start(out=x_raw[c][cut][:], in_=x_rows[c][:, :, cut_cols])
         for c in range(PASSES):
             nc.sync.dma_start(out=g_rest[c][:], in_=g_rows[c][:, :, PIECE:DOUT])
 
@@ -95,27 +102,32 @@ def tile_linearmem_kernel(tc, x, weight, bias, grad_out, out):
             for n in range(N_TILES):
                 copy = nc.vector.tensor_copy if n == N_TILES - 1 else nc.scalar.copy
                 copy(out=out_rows[:, n * N_TILE : (n + 1) * N_TILE], in_=banks[n][:])
-            nc.sync.dma_start(out=out[m * M_TILE : (m + 1) * M_TILE, :], in_=out_rows[:])
+            if m >= M_TILES - 2:
+                for n in range(N_TILES):
+                    n_cols = slice(n * N_TILE, (n + 1) * N_TILE)
+                    nc.sync.dma_start(out=out[m * M_TILE : (m + 1) * M_TILE, n_cols], in_=out_rows[:, n_cols])
+            else:
+                nc.sync.dma_start(out=out[m * M_TILE : (m + 1) * M_TILE, :], in_=out_rows[:])
             piece, c = m // M_TILES_PER_PIECE + 1, m % M_TILES_PER_PIECE - 1
             if piece < G_PIECES and c in range(PASSES):
                 quantise(regroup(nc.vector.tensor_copy, g_piece_rows(piece, c)), g_codes, g_scales, piece, c, E5M2_X4)
 
         copies = (nc.vector.tensor_copy, nc.scalar.copy)
         g_grouped = [regroup(copies[c], g_piece_rows(0, c)) for c in range(PASSES)]
-        for c in range(PASSES):
-            quantise(g_grouped[c], g_codes, g_scales, 0, c, E5M2_X4)
 
         early_banks = [open_banks() for m in range(EARLY)]
         for c in range(PASSES):
-            x_grouped = [
-                regroup(copies[piece % 2], x_raw[c][:, :, piece * PIECE : (piece + 1) * PIECE])
-                for piece in range(X_PIECES)
-            ]
-            for piece in range(X_PIECES):
-                quantise(x_grouped[piece], x_codes, x_scales, piece, c, E4M3_X4)
-            for n in range(N_TILES):
-                for m in range(EARLY):
-                    multiply(early_banks[m], m, n, c)
+            quantise(g_grouped[c], g_codes, g_scales, 0, c, E5M2_X4)
+            for cut in range(X_CUTS):
+                x_grouped = [
+                    regroup(copies[i % 2], x_raw[c][cut][:, :, i * PIECE : (i + 1) * PIECE])
+                    for i in range(X_PIECES_PER_CUT)
+                ]
+                for i in range(X_PIECES_PER_CUT):
+                    n = cut * X_PIECES_PER_CUT + i
+                    quantise(x_grouped[i], x_codes, x_scales, n, c, E4M3_X4)
+                    for m in range(EARLY):
+                        multiply(early_banks[m], m, n, c)
         for m in range(EARLY):
             finish(early_banks[m], m)
 

@@ -52,8 +52,8 @@ def tile_linearmem_kernel(tc, x, weight, bias, grad_out, out):
         g_rest = [raw.tile([P, PACK, DOUT - PIECE], BF16, name="g_rest%d" % c) for c in range(PASSES)]
         for c in range(PASSES):
             nc.sync.dma_start(out=g_first[c][:], in_=g_rows[c][:, :, 0:PIECE])
-        for c in range(PASSES):
-            for cut in range(X_CUTS):
+        for cut in range(X_CUTS):
+            for c in range(PASSES):
                 cut_cols = slice(cut * (DIN // X_CUTS), (cut + 1) * (DIN // X_CUTS))
                 nc.sync.dma_start(out=x_raw[c][cut][:], in_=x_rows[c][:, :, cut_cols])
         for c in range(PASSES):
@@ -112,26 +112,94 @@ def tile_linearmem_kernel(tc, x, weight, bias, grad_out, out):
             if piece < G_PIECES and c in range(PASSES):
                 quantise(regroup(nc.vector.tensor_copy, g_piece_rows(piece, c)), g_codes, g_scales, piece, c, E5M2_X4)
 
-        copies = (nc.vector.tensor_copy, nc.scalar.copy)
-        g_grouped = [regroup(copies[c], g_piece_rows(0, c)) for c in range(PASSES)]
+        V, S = nc.vector.tensor_copy, nc.scalar.copy
 
-        early_banks = [open_banks() for m in range(EARLY)]
-        for c in range(PASSES):
-            quantise(g_grouped[c], g_codes, g_scales, 0, c, E5M2_X4)
-            for cut in range(X_CUTS):
-                x_grouped = [
-                    regroup(copies[i % 2], x_raw[c][cut][:, :, i * PIECE : (i + 1) * PIECE])
-                    for i in range(X_PIECES_PER_CUT)
-                ]
-                for i in range(X_PIECES_PER_CUT):
-                    n = cut * X_PIECES_PER_CUT + i
-                    quantise(x_grouped[i], x_codes, x_scales, n, c, E4M3_X4)
-                    for m in range(EARLY):
-                        multiply(early_banks[m], m, n, c)
-        for m in range(EARLY):
-            finish(early_banks[m], m)
+        def x_piece_rows(n, c):
+            cut, i = divmod(n, X_PIECES_PER_CUT)
+            return x_raw[c][cut][:, :, i * PIECE : (i + 1) * PIECE]
 
-        for m in range(EARLY, M_TILES):
+        def x_quantise(grouped, n, c):
+            quantise(grouped, x_codes, x_scales, n, c, E4M3_X4)
+
+        HEAD_TILES = M_TILES_PER_PIECE
+        head_rows = [result.tile([P, DIN], F32, name="out_rows") for m in range(HEAD_TILES)]
+        head_banks = {}
+
+        def head_open(n):
+            head_banks[n] = [psum.tile([P, N_TILE], F32, name="bank") for m in range(HEAD_TILES)]
+
+        def head_multiply(n, c):
+            for m in range(HEAD_TILES):
+                nc.tensor.matmul_mx(
+                    out=head_banks[n][m][:],
+                    lhsT=g_codes[:, c, m * M_TILE : (m + 1) * M_TILE].bitcast(E5M2_X4),
+                    lhsT_scale=g_scales[:, c, m * M_TILE : (m + 1) * M_TILE],
+                    rhs=x_codes[:, c, n * N_TILE : (n + 1) * N_TILE].bitcast(E4M3_X4),
+                    rhs_scale=x_scales[:, c, n * N_TILE : (n + 1) * N_TILE],
+                    start=(c == 0),
+                    stop=(c == PASSES - 1),
+                )
+
+        def head_empty(copy, n, m):
+            copy(out=head_rows[m][:, n * N_TILE : (n + 1) * N_TILE], in_=head_banks[n][m][:])
+
+        def head_store(m, half):
+            cols = slice(half * (DIN // 2), (half + 1) * (DIN // 2))
+            nc.sync.dma_start(out=out[m * M_TILE : (m + 1) * M_TILE, cols], in_=head_rows[m][:, cols])
+
+        g0c0 = regroup(V, g_piece_rows(0, 0))
+        g0c1 = regroup(S, g_piece_rows(0, 1))
+        quantise(g0c0, g_codes, g_scales, 0, 0, E5M2_X4)
+        n0c0 = regroup(V, x_piece_rows(0, 0))
+        n1c0 = regroup(S, x_piece_rows(1, 0))
+        quantise(g0c1, g_codes, g_scales, 0, 1, E5M2_X4)
+        x_quantise(n0c0, 0, 0)
+        head_open(0)
+        head_multiply(0, 0)
+        n0c1 = regroup(V, x_piece_rows(0, 1))
+        n1c1 = regroup(S, x_piece_rows(1, 1))
+        x_quantise(n1c0, 1, 0)
+        head_open(1)
+        head_multiply(1, 0)
+        x_quantise(n0c1, 0, 1)
+        head_multiply(0, 1)
+        n2c0 = regroup(V, x_piece_rows(2, 0))
+        x_quantise(n1c1, 1, 1)
+        head_multiply(1, 1)
+        for m in range(HEAD_TILES):
+            head_empty(S, 0, m)
+        n3c0 = regroup(V, x_piece_rows(3, 0))
+        x_quantise(n2c0, 2, 0)
+        head_open(2)
+        head_multiply(2, 0)
+        for m in range(HEAD_TILES):
+            head_empty(S, 1, m)
+            head_store(m, 0)
+        n2c1 = regroup(V, x_piece_rows(2, 1))
+        x_quantise(n3c0, 3, 0)
+        head_open(3)
+        head_multiply(3, 0)
+        n3c1 = regroup(V, x_piece_rows(3, 1))
+        x_quantise(n2c1, 2, 1)
+        head_multiply(2, 1)
+        x_quantise(n3c1, 3, 1)
+        head_multiply(3, 1)
+        g1c0 = regroup(V, g_piece_rows(1, 0))
+        g1c1 = regroup(V, g_piece_rows(1, 1))
+        head_empty(S, 2, 0)
+        head_empty(S, 2, 1)
+        quantise(g1c0, g_codes, g_scales, 1, 0, E5M2_X4)
+        quantise(g1c1, g_codes, g_scales, 1, 1, E5M2_X4)
+        head_empty(S, 3, 0)
+        head_store(0, 1)
+        head_empty(S, 3, 1)
+        head_store(1, 1)
+        for m in range(2, HEAD_TILES):
+            head_empty(S, 2, m)
+            head_empty(S, 3, m)
+            head_store(m, 1)
+
+        for m in range(HEAD_TILES, M_TILES):
             banks = open_banks()
             for c in range(PASSES):
                 for n in range(N_TILES):

@@ -102,12 +102,7 @@ def tile_linearmem_kernel(tc, x, weight, bias, grad_out, out):
             for n in range(N_TILES):
                 copy = nc.vector.tensor_copy if n == N_TILES - 1 else nc.scalar.copy
                 copy(out=out_rows[:, n * N_TILE : (n + 1) * N_TILE], in_=banks[n][:])
-            if m >= M_TILES - 2:
-                for n in range(N_TILES):
-                    n_cols = slice(n * N_TILE, (n + 1) * N_TILE)
-                    nc.sync.dma_start(out=out[m * M_TILE : (m + 1) * M_TILE, n_cols], in_=out_rows[:, n_cols])
-            else:
-                nc.sync.dma_start(out=out[m * M_TILE : (m + 1) * M_TILE, :], in_=out_rows[:])
+            nc.sync.dma_start(out=out[m * M_TILE : (m + 1) * M_TILE, :], in_=out_rows[:])
             piece, c = m // M_TILES_PER_PIECE + 1, m % M_TILES_PER_PIECE - 1
             if piece < G_PIECES and c in range(PASSES):
                 quantise(regroup(nc.vector.tensor_copy, g_piece_rows(piece, c)), g_codes, g_scales, piece, c, E5M2_X4)

@@ -100,9 +100,10 @@ def tile_linearmem_kernel(tc, x, weight, bias, grad_out, out):
         def finish(banks, m):
             out_rows = result.tile([P, DIN], F32, name="out_rows")
             for n in range(N_TILES):
-                copy = nc.vector.tensor_copy if n == N_TILES - 1 else nc.scalar.copy
+                copy = nc.vector.tensor_copy if n == N_TILES - 1 and m % 2 == 0 else nc.scalar.copy
                 copy(out=out_rows[:, n * N_TILE : (n + 1) * N_TILE], in_=banks[n][:])
-            nc.sync.dma_start(out=out[m * M_TILE : (m + 1) * M_TILE, :], in_=out_rows[:])
+            queue = nc.sync if m % 2 == 0 else nc.scalar
+            queue.dma_start(out=out[m * M_TILE : (m + 1) * M_TILE, :], in_=out_rows[:])
             piece, c = m // M_TILES_PER_PIECE + 1, m % M_TILES_PER_PIECE - 1
             if piece < G_PIECES and c in range(PASSES):
                 quantise(regroup(nc.vector.tensor_copy, g_piece_rows(piece, c)), g_codes, g_scales, piece, c, E5M2_X4)

@@ -102,8 +102,7 @@ def tile_linearmem_kernel(tc, x, weight, bias, grad_out, out):
             for n in range(N_TILES):
                 copy = nc.vector.tensor_copy if n == N_TILES - 1 and m % 2 == 0 else nc.scalar.copy
                 copy(out=out_rows[:, n * N_TILE : (n + 1) * N_TILE], in_=banks[n][:])
-            queue = nc.sync if m % 2 == 0 else nc.scalar
-            queue.dma_start(out=out[m * M_TILE : (m + 1) * M_TILE, :], in_=out_rows[:])
+            nc.sync.dma_start(out=out[m * M_TILE : (m + 1) * M_TILE, :], in_=out_rows[:])
             piece, c = m // M_TILES_PER_PIECE + 1, m % M_TILES_PER_PIECE - 1
             if piece < G_PIECES and c in range(PASSES):
                 quantise(regroup(nc.vector.tensor_copy, g_piece_rows(piece, c)), g_codes, g_scales, piece, c, E5M2_X4)

@@ -100,8 +100,7 @@ def tile_linearmem_kernel(tc, x, weight, bias, grad_out, out):
         def finish(banks, m):
             out_rows = result.tile([P, DIN], F32, name="out_rows")
             for n in range(N_TILES):
-                copy = nc.vector.tensor_copy if n == N_TILES - 1 and m % 2 == 0 else nc.scalar.copy
-                copy(out=out_rows[:, n * N_TILE : (n + 1) * N_TILE], in_=banks[n][:])
+                nc.scalar.copy(out=out_rows[:, n * N_TILE : (n + 1) * N_TILE], in_=banks[n][:])
             nc.sync.dma_start(out=out[m * M_TILE : (m + 1) * M_TILE, :], in_=out_rows[:])
             piece, c = m // M_TILES_PER_PIECE + 1, m % M_TILES_PER_PIECE - 1
             if piece < G_PIECES and c in range(PASSES):

@@ -40,7 +40,8 @@ def tile_linearmem_kernel(tc, x, weight, bias, grad_out, out):
         raw = ctx.enter_context(tc.tile_pool(name="raw", bufs=1))
         keep = ctx.enter_context(tc.tile_pool(name="keep", bufs=1))
         stage = ctx.enter_context(tc.tile_pool(name="stage", bufs=6))
-        result = ctx.enter_context(tc.tile_pool(name="result", bufs=8))
+        head_pool = ctx.enter_context(tc.tile_pool(name="head", bufs=1))
+        result = ctx.enter_context(tc.tile_pool(name="result", bufs=6))
         psum = ctx.enter_context(tc.psum_pool(name="psum", bufs=PSUM_BANKS))
         ctx.enter_context(tc.manual_schedule())
 
@@ -116,7 +117,9 @@ def tile_linearmem_kernel(tc, x, weight, bias, grad_out, out):
             quantise(grouped, x_codes, x_scales, n, c, E4M3_X4)
 
         HEAD_TILES = M_TILES_PER_PIECE
-        head_rows = [result.tile([P, DIN], F32, name="out_rows") for m in range(HEAD_TILES)]
+        HALF = DIN // 2
+        head_left = head_pool.tile([P, HEAD_TILES, HALF], F32, name="head_left")
+        head_right = [head_pool.tile([P, 2, HALF], F32, name="head_right%d" % k) for k in range(HEAD_TILES // 2)]
         head_banks = {}
 
         def head_open(n):
@@ -135,11 +138,20 @@ def tile_linearmem_kernel(tc, x, weight, bias, grad_out, out):
                 )
 
         def head_empty(copy, n, m):
-            copy(out=head_rows[m][:, n * N_TILE : (n + 1) * N_TILE], in_=head_banks[n][m][:])
+            cols = slice(n % 2 * N_TILE, (n % 2 + 1) * N_TILE)
+            rows = head_left[:, m, cols] if n < 2 else head_right[m // 2][:, m % 2, cols]
+            copy(out=rows, in_=head_banks[n][m][:])
 
         def head_store(m, half):
-            cols = slice(half * (DIN // 2), (half + 1) * (DIN // 2))
-            nc.sync.dma_start(out=out[m * M_TILE : (m + 1) * M_TILE, cols], in_=head_rows[m][:, cols])
+            if half == 0 and m == HEAD_TILES - 1:
+                nc.sync.dma_start(
+                    out=out[0 : HEAD_TILES * M_TILE, 0:HALF].rearrange("(t p) d -> p t d", p=P), in_=head_left[:]
+                )
+            if half == 1 and m % 2 == 1:
+                nc.sync.dma_start(
+                    out=out[(m - 1) * M_TILE : (m + 1) * M_TILE, HALF:DIN].rearrange("(t p) d -> p t d", p=P),
+                    in_=head_right[m // 2][:],
+                )
 
         g0c0 = regroup(V, g_piece_rows(0, 0))
         g0c1 = regroup(S, g_piece_rows(0, 1))

@@ -19,13 +19,9 @@ N_TILE = 512
 M_TILES = DOUT // M_TILE
 N_TILES = DIN // N_TILE
 PSUM_BANKS = 8
-EARLY = PSUM_BANKS // N_TILES
 PIECE = 512
-M_TILES_PER_PIECE = PIECE // M_TILE
-G_PIECES = DOUT // PIECE
-X_PIECES = DIN // PIECE
-X_CUTS = 2
-X_PIECES_PER_CUT = X_PIECES // X_CUTS
+M_PER_PIECE = PIECE // M_TILE
+HALF = DIN // 2
 
 FLOPS = 2 * PASSES * P * PACK * DIN * DOUT
 BYTES = 2 * PASSES * P * PACK * (DIN + DOUT) + 4 * DIN * DOUT
@@ -40,174 +36,152 @@ def tile_linearmem_kernel(tc, x, weight, bias, grad_out, out):
         raw = ctx.enter_context(tc.tile_pool(name="raw", bufs=1))
         keep = ctx.enter_context(tc.tile_pool(name="keep", bufs=1))
         stage = ctx.enter_context(tc.tile_pool(name="stage", bufs=6))
-        head_pool = ctx.enter_context(tc.tile_pool(name="head", bufs=1))
         result = ctx.enter_context(tc.tile_pool(name="result", bufs=6))
         psum = ctx.enter_context(tc.psum_pool(name="psum", bufs=PSUM_BANKS))
         ctx.enter_context(tc.manual_schedule())
 
-        x_raw = [
-            [raw.tile([P, PACK, DIN // X_CUTS], BF16, name="x_raw%d_%d" % (c, cut)) for cut in range(X_CUTS)]
-            for c in range(PASSES)
-        ]
-        g_first = [raw.tile([P, PACK, PIECE], BF16, name="g_first%d" % c) for c in range(PASSES)]
-        g_rest = [raw.tile([P, PACK, DOUT - PIECE], BF16, name="g_rest%d" % c) for c in range(PASSES)]
-        for c in range(PASSES):
-            nc.sync.dma_start(out=g_first[c][:], in_=g_rows[c][:, :, 0:PIECE])
-        for cut in range(X_CUTS):
-            for c in range(PASSES):
-                cut_cols = slice(cut * (DIN // X_CUTS), (cut + 1) * (DIN // X_CUTS))
-                nc.sync.dma_start(out=x_raw[c][cut][:], in_=x_rows[c][:, :, cut_cols])
-        for c in range(PASSES):
-            nc.sync.dma_start(out=g_rest[c][:], in_=g_rows[c][:, :, PIECE:DOUT])
+        raw_pieces = {}
 
-        x_codes = keep.tile([P, PASSES, DIN], U32, align_bytes=64)
-        x_scales = keep.tile([P, PASSES, DIN], U8, align_bytes=64)
-        g_codes = keep.tile([P, PASSES, DOUT], U32, align_bytes=64)
-        g_scales = keep.tile([P, PASSES, DOUT], U8, align_bytes=64)
+        def load(which, rows, c, first, width):
+            tile = raw.tile([P, PACK, width], BF16, name="raw_%s%d_%d" % (which, c, first))
+            nc.sync.dma_start(out=tile[:], in_=rows[c][:, :, first : first + width])
+            for piece in range(first // PIECE, (first + width) // PIECE):
+                at = piece * PIECE - first
+                raw_pieces[which, piece, c] = tile[:, :, at : at + PIECE]
 
-        def regroup(copy, rows):
+        for c in range(PASSES):
+            load("g", g_rows, c, 0, PIECE)
+        for c in range(PASSES):
+            load("x", x_rows, c, 0, HALF)
+        for c in range(PASSES):
+            load("g", g_rows, c, PIECE, PIECE)
+        for c in range(PASSES):
+            load("x", x_rows, c, HALF, HALF)
+        for c in range(PASSES):
+            load("g", g_rows, c, HALF, HALF)
+
+        codes = {
+            "x": keep.tile([P, PASSES, DIN], U32, align_bytes=64, name="x_codes"),
+            "g": keep.tile([P, PASSES, DOUT], U32, align_bytes=64, name="g_codes"),
+        }
+        scales = {
+            "x": keep.tile([P, PASSES, DIN], U8, align_bytes=64, name="x_scales"),
+            "g": keep.tile([P, PASSES, DOUT], U8, align_bytes=64, name="g_scales"),
+        }
+        packed = {"x": E4M3_X4, "g": E5M2_X4}
+        grouped_pieces = {}
+
+        def regroup(copy, which, piece, c):
             grouped = stage.tile([P, PIECE, PACK], BF16, align_bytes=64, name="grouped")
             copy(
                 out=grouped[:].rearrange("p (v i) j -> p v j i", i=4),
-                in_=rows.rearrange("p j (v i) -> p v j i", i=4),
+                in_=raw_pieces[which, piece, c].rearrange("p j (v i) -> p v j i", i=4),
             )
-            return grouped
+            grouped_pieces[which, piece, c] = grouped
 
-        def quantise(grouped, codes, scales, piece, c, packed_dtype):
+        def quantise(which, piece, c):
             cols = slice(piece * PIECE, (piece + 1) * PIECE)
             nc.vector.quantize_mx(
-                out=codes[:, c, cols].bitcast(packed_dtype),
-                scales=scales[:, c, cols],
-                in_=grouped[:].rearrange("p v j -> p (v j)"),
+                out=codes[which][:, c, cols].bitcast(packed[which]),
+                scales=scales[which][:, c, cols],
+                in_=grouped_pieces[which, piece, c][:].rearrange("p v j -> p (v j)"),
             )
 
-        def g_piece_rows(piece, c):
-            return g_first[c][:] if piece == 0 else g_rest[c][:, :, (piece - 1) * PIECE : piece * PIECE]
+        banks = {}
 
-        def multiply(banks, m, n, c):
+        def multiply(m, n, c):
+            if c == 0:
+                banks[m, n] = psum.tile([P, N_TILE], F32, name="bank")
+            m_cols = slice(m * M_TILE, (m + 1) * M_TILE)
+            n_cols = slice(n * N_TILE, (n + 1) * N_TILE)
             nc.tensor.matmul_mx(
-                out=banks[n][:],
-                lhsT=g_codes[:, c, m * M_TILE : (m + 1) * M_TILE].bitcast(E5M2_X4),
-                lhsT_scale=g_scales[:, c, m * M_TILE : (m + 1) * M_TILE],
-                rhs=x_codes[:, c, n * N_TILE : (n + 1) * N_TILE].bitcast(E4M3_X4),
-                rhs_scale=x_scales[:, c, n * N_TILE : (n + 1) * N_TILE],
+                out=banks[m, n][:],
+                lhsT=codes["g"][:, c, m_cols].bitcast(E5M2_X4),
+                lhsT_scale=scales["g"][:, c, m_cols],
+                rhs=codes["x"][:, c, n_cols].bitcast(E4M3_X4),
+                rhs_scale=scales["x"][:, c, n_cols],
                 start=(c == 0),
                 stop=(c == PASSES - 1),
             )
 
-        def open_banks():
-            return [psum.tile([P, N_TILE], F32, name="bank") for n in range(N_TILES)]
-
-        def finish(banks, m):
-            out_rows = result.tile([P, DIN], F32, name="out_rows")
-            for n in range(N_TILES):
-                nc.scalar.copy(out=out_rows[:, n * N_TILE : (n + 1) * N_TILE], in_=banks[n][:])
-            nc.sync.dma_start(out=out[m * M_TILE : (m + 1) * M_TILE, :], in_=out_rows[:])
-            piece, c = m // M_TILES_PER_PIECE + 1, m % M_TILES_PER_PIECE - 1
-            if piece < G_PIECES and c in range(PASSES):
-                quantise(regroup(nc.vector.tensor_copy, g_piece_rows(piece, c)), g_codes, g_scales, piece, c, E5M2_X4)
-
         V, S = nc.vector.tensor_copy, nc.scalar.copy
 
-        def x_piece_rows(n, c):
-            cut, i = divmod(n, X_PIECES_PER_CUT)
-            return x_raw[c][cut][:, :, i * PIECE : (i + 1) * PIECE]
+        def multiply_piece(g_piece, n, c):
+            for m in range(g_piece * M_PER_PIECE, (g_piece + 1) * M_PER_PIECE):
+                multiply(m, n, c)
 
-        def x_quantise(grouped, n, c):
-            quantise(grouped, x_codes, x_scales, n, c, E4M3_X4)
+        def empty_quarter(g_piece, half):
+            rows = result.tile([P, M_PER_PIECE, HALF], F32, name="rows")
+            for n in range(2):
+                for t in range(M_PER_PIECE):
+                    S(
+                        out=rows[:, t, n * N_TILE : (n + 1) * N_TILE],
+                        in_=banks[g_piece * M_PER_PIECE + t, 2 * half + n][:],
+                    )
+            nc.sync.dma_start(
+                out=out[g_piece * PIECE : (g_piece + 1) * PIECE, half * HALF : (half + 1) * HALF].rearrange(
+                    "(t p) d -> p t d", p=P
+                ),
+                in_=rows[:],
+            )
 
-        HEAD_TILES = M_TILES_PER_PIECE
-        HALF = DIN // 2
-        head_left = head_pool.tile([P, HEAD_TILES, HALF], F32, name="head_left")
-        head_right = [head_pool.tile([P, 2, HALF], F32, name="head_right%d" % k) for k in range(HEAD_TILES // 2)]
-        head_banks = {}
+        regroup(V, "g", 0, 0)
+        regroup(S, "g", 0, 1)
+        quantise("g", 0, 0)
+        regroup(V, "x", 0, 0)
+        regroup(S, "x", 1, 0)
+        quantise("g", 0, 1)
+        quantise("x", 0, 0)
+        multiply_piece(0, 0, 0)
+        regroup(V, "x", 0, 1)
+        regroup(S, "x", 1, 1)
+        quantise("x", 1, 0)
+        multiply_piece(0, 1, 0)
+        quantise("x", 0, 1)
+        multiply_piece(0, 0, 1)
+        regroup(V, "g", 1, 0)
+        quantise("x", 1, 1)
+        multiply_piece(0, 1, 1)
+        empty_quarter(0, 0)
 
-        def head_open(n):
-            head_banks[n] = [psum.tile([P, N_TILE], F32, name="bank") for m in range(HEAD_TILES)]
+        regroup(V, "g", 1, 1)
+        quantise("g", 1, 0)
+        multiply_piece(1, 0, 0)
+        quantise("g", 1, 1)
+        multiply_piece(1, 0, 1)
+        for c in range(PASSES):
+            multiply_piece(1, 1, c)
+        empty_quarter(1, 0)
 
-        def head_multiply(n, c):
-            for m in range(HEAD_TILES):
-                nc.tensor.matmul_mx(
-                    out=head_banks[n][m][:],
-                    lhsT=g_codes[:, c, m * M_TILE : (m + 1) * M_TILE].bitcast(E5M2_X4),
-                    lhsT_scale=g_scales[:, c, m * M_TILE : (m + 1) * M_TILE],
-                    rhs=x_codes[:, c, n * N_TILE : (n + 1) * N_TILE].bitcast(E4M3_X4),
-                    rhs_scale=x_scales[:, c, n * N_TILE : (n + 1) * N_TILE],
-                    start=(c == 0),
-                    stop=(c == PASSES - 1),
-                )
-
-        def head_empty(copy, n, m):
-            cols = slice(n % 2 * N_TILE, (n % 2 + 1) * N_TILE)
-            rows = head_left[:, m, cols] if n < 2 else head_right[m // 2][:, m % 2, cols]
-            copy(out=rows, in_=head_banks[n][m][:])
-
-        def head_store(m, half):
-            if half == 0 and m == HEAD_TILES - 1:
-                nc.sync.dma_start(
-                    out=out[0 : HEAD_TILES * M_TILE, 0:HALF].rearrange("(t p) d -> p t d", p=P), in_=head_left[:]
-                )
-            if half == 1 and m % 2 == 1:
-                nc.sync.dma_start(
-                    out=out[(m - 1) * M_TILE : (m + 1) * M_TILE, HALF:DIN].rearrange("(t p) d -> p t d", p=P),
-                    in_=head_right[m // 2][:],
-                )
-
-        g0c0 = regroup(V, g_piece_rows(0, 0))
-        g0c1 = regroup(S, g_piece_rows(0, 1))
-        quantise(g0c0, g_codes, g_scales, 0, 0, E5M2_X4)
-        n0c0 = regroup(V, x_piece_rows(0, 0))
-        n1c0 = regroup(S, x_piece_rows(1, 0))
-        quantise(g0c1, g_codes, g_scales, 0, 1, E5M2_X4)
-        x_quantise(n0c0, 0, 0)
-        head_open(0)
-        head_multiply(0, 0)
-        n0c1 = regroup(V, x_piece_rows(0, 1))
-        n1c1 = regroup(S, x_piece_rows(1, 1))
-        x_quantise(n1c0, 1, 0)
-        head_open(1)
-        head_multiply(1, 0)
-        x_quantise(n0c1, 0, 1)
-        head_multiply(0, 1)
-        n2c0 = regroup(V, x_piece_rows(2, 0))
-        x_quantise(n1c1, 1, 1)
-        head_multiply(1, 1)
-        for m in range(HEAD_TILES):
-            head_empty(S, 0, m)
-        n3c0 = regroup(V, x_piece_rows(3, 0))
-        x_quantise(n2c0, 2, 0)
-        head_open(2)
-        head_multiply(2, 0)
-        for m in range(HEAD_TILES):
-            head_empty(S, 1, m)
-            head_store(m, 0)
-        n2c1 = regroup(V, x_piece_rows(2, 1))
-        x_quantise(n3c0, 3, 0)
-        head_open(3)
-        head_multiply(3, 0)
-        n3c1 = regroup(V, x_piece_rows(3, 1))
-        x_quantise(n2c1, 2, 1)
-        head_multiply(2, 1)
-        x_quantise(n3c1, 3, 1)
-        head_multiply(3, 1)
-        g1c0 = regroup(V, g_piece_rows(1, 0))
-        g1c1 = regroup(V, g_piece_rows(1, 1))
-        head_empty(S, 2, 0)
-        head_empty(S, 2, 1)
-        quantise(g1c0, g_codes, g_scales, 1, 0, E5M2_X4)
-        quantise(g1c1, g_codes, g_scales, 1, 1, E5M2_X4)
-        head_empty(S, 3, 0)
-        head_store(0, 1)
-        head_empty(S, 3, 1)
-        head_store(1, 1)
-        for m in range(2, HEAD_TILES):
-            head_empty(S, 2, m)
-            head_empty(S, 3, m)
-            head_store(m, 1)
-
-        for m in range(HEAD_TILES, M_TILES):
-            banks = open_banks()
+        for n in (2, 3):
+            regroup(V, "x", n, 0)
+            regroup(V, "x", n, 1)
+            quantise("x", n, 0)
+            multiply_piece(0, n, 0)
+            quantise("x", n, 1)
+            multiply_piece(0, n, 1)
+        empty_quarter(0, 1)
+        for n in (2, 3):
             for c in range(PASSES):
+                multiply_piece(1, n, c)
+        empty_quarter(1, 1)
+
+        for piece in (2, 3):
+            regroup(V, "g", piece, 0)
+            regroup(V, "g", piece, 1)
+            quantise("g", piece, 0)
+            quantise("g", piece, 1)
+
+        for pair in range(M_TILES // 4, M_TILES // 2):
+            rows = result.tile([P, 2, DIN], F32, name="rows")
+            for t in range(2):
+                m = 2 * pair + t
+                for c in range(PASSES):
+                    for n in range(N_TILES):
+                        multiply(m, n, c)
                 for n in range(N_TILES):
-                    multiply(banks, m, n, c)
-            finish(banks, m)
+                    copy = V if n % 2 == 1 and pair > M_TILES // 4 else S
+                    copy(out=rows[:, t, n * N_TILE : (n + 1) * N_TILE], in_=banks[m, n][:])
+            nc.sync.dma_start(
+                out=out[2 * pair * M_TILE : 2 * (pair + 1) * M_TILE, :].rearrange("(t p) d -> p t d", p=P), in_=rows[:]
+            )

@@ -73,9 +73,10 @@ def tile_linearmem_kernel(tc, x, weight, bias, grad_out, out):
 
         def regroup(copy, which, piece, c):
             grouped = stage.tile([P, PIECE, PACK], BF16, align_bytes=64, name="grouped")
+            order = "p (t m) j -> p m j t" if which == "g" else "p (m t) j -> p m j t"
             copy(
-                out=grouped[:].rearrange("p (v i) j -> p v j i", i=4),
-                in_=raw_pieces[which, piece, c].rearrange("p j (v i) -> p v j i", i=4),
+                out=grouped[:].rearrange(order, t=4),
+                in_=raw_pieces[which, piece, c].rearrange("p j (m t) -> p m j t", t=4),
             )
             grouped_pieces[which, piece, c] = grouped
 
@@ -120,7 +121,7 @@ def tile_linearmem_kernel(tc, x, weight, bias, grad_out, out):
                     )
             nc.sync.dma_start(
                 out=out[g_piece * PIECE : (g_piece + 1) * PIECE, half * HALF : (half + 1) * HALF].rearrange(
-                    "(t p) d -> p t d", p=P
+                    "(p t) d -> p t d", p=P
                 ),
                 in_=rows[:],
             )
@@ -182,6 +183,5 @@ def tile_linearmem_kernel(tc, x, weight, bias, grad_out, out):
                 for n in range(N_TILES):
                     copy = V if n % 2 == 1 and pair > M_TILES // 4 else S
                     copy(out=rows[:, t, n * N_TILE : (n + 1) * N_TILE], in_=banks[m, n][:])
-            nc.sync.dma_start(
-                out=out[2 * pair * M_TILE : 2 * (pair + 1) * M_TILE, :].rearrange("(t p) d -> p t d", p=P), in_=rows[:]
-            )
+            piece_rows = out[pair // 2 * PIECE : (pair // 2 + 1) * PIECE, :].rearrange("(p t) d -> p t d", p=P)
+            nc.sync.dma_start(out=piece_rows[:, pair % 2 * 2 : pair % 2 * 2 + 2, :], in_=rows[:])

@@ -111,14 +111,20 @@ def tile_linearmem_kernel(tc, x, weight, bias, grad_out, out):
             for m in range(g_piece * M_PER_PIECE, (g_piece + 1) * M_PER_PIECE):
                 multiply(m, n, c)
 
-        def empty_quarter(g_piece, half):
+        def multiply_quarter(g_piece, half):
+            for m in range(g_piece * M_PER_PIECE, (g_piece + 1) * M_PER_PIECE):
+                for c in range(PASSES):
+                    for n in (2 * half, 2 * half + 1):
+                        multiply(m, n, c)
+
+        def empty_quarter(g_piece, half, by_rows):
             rows = result.tile([P, M_PER_PIECE, HALF], F32, name="rows")
-            for n in range(2):
-                for t in range(M_PER_PIECE):
-                    S(
-                        out=rows[:, t, n * N_TILE : (n + 1) * N_TILE],
-                        in_=banks[g_piece * M_PER_PIECE + t, 2 * half + n][:],
-                    )
+            by_columns = [(t, n) for n in range(2) for t in range(M_PER_PIECE)]
+            for t, n in sorted(by_columns) if by_rows else by_columns:
+                S(
+                    out=rows[:, t, n * N_TILE : (n + 1) * N_TILE],
+                    in_=banks[g_piece * M_PER_PIECE + t, 2 * half + n][:],
+                )
             nc.sync.dma_start(
                 out=out[g_piece * PIECE : (g_piece + 1) * PIECE, half * HALF : (half + 1) * HALF].rearrange(
                     "(p t) d -> p t d", p=P
@@ -143,16 +149,13 @@ def tile_linearmem_kernel(tc, x, weight, bias, grad_out, out):
         regroup(V, "g", 1, 0)
         quantise("x", 1, 1)
         multiply_piece(0, 1, 1)
-        empty_quarter(0, 0)
+        empty_quarter(0, 0, False)
 
         regroup(V, "g", 1, 1)
         quantise("g", 1, 0)
-        multiply_piece(1, 0, 0)
         quantise("g", 1, 1)
-        multiply_piece(1, 0, 1)
-        for c in range(PASSES):
-            multiply_piece(1, 1, c)
-        empty_quarter(1, 0)
+        multiply_quarter(1, 0)
+        empty_quarter(1, 0, True)
 
         for n in (2, 3):
             regroup(V, "x", n, 0)
@@ -161,11 +164,9 @@ def tile_linearmem_kernel(tc, x, weight, bias, grad_out, out):
             multiply_piece(0, n, 0)
             quantise("x", n, 1)
             multiply_piece(0, n, 1)
-        empty_quarter(0, 1)
-        for n in (2, 3):
-            for c in range(PASSES):
-                multiply_piece(1, n, c)
-        empty_quarter(1, 1)
+        empty_quarter(0, 1, False)
+        multiply_quarter(1, 1)
+        empty_quarter(1, 1, True)
 
         for piece in (2, 3):
             regroup(V, "g", piece, 0)

@@ -50,11 +50,8 @@ def tile_linearmem_kernel(tc, x, weight, bias, grad_out, out):
                 raw_pieces[which, piece, c] = tile[:, :, at : at + PIECE]
 
         for c in range(PASSES):
-            load("g", g_rows, c, 0, PIECE)
-        for c in range(PASSES):
             load("x", x_rows, c, 0, HALF)
-        for c in range(PASSES):
-            load("g", g_rows, c, PIECE, PIECE)
+            load("g", g_rows, c, 0, HALF)
         for c in range(PASSES):
             load("x", x_rows, c, HALF, HALF)
         for c in range(PASSES):
@@ -117,45 +114,46 @@ def tile_linearmem_kernel(tc, x, weight, bias, grad_out, out):
                     for n in (2 * half, 2 * half + 1):
                         multiply(m, n, c)
 
-        def empty_quarter(g_piece, half, by_rows):
+        def empty_quarter(g_piece, half, by_rows, stores):
             rows = result.tile([P, M_PER_PIECE, HALF], F32, name="rows")
+            piece_rows = out[g_piece * PIECE : (g_piece + 1) * PIECE, half * HALF : (half + 1) * HALF].rearrange(
+                "(p t) d -> p t d", p=P
+            )
             by_columns = [(t, n) for n in range(2) for t in range(M_PER_PIECE)]
+            tiles = M_PER_PIECE // stores
             for t, n in sorted(by_columns) if by_rows else by_columns:
                 S(
                     out=rows[:, t, n * N_TILE : (n + 1) * N_TILE],
                     in_=banks[g_piece * M_PER_PIECE + t, 2 * half + n][:],
                 )
-            nc.sync.dma_start(
-                out=out[g_piece * PIECE : (g_piece + 1) * PIECE, half * HALF : (half + 1) * HALF].rearrange(
-                    "(p t) d -> p t d", p=P
-                ),
-                in_=rows[:],
-            )
+                if n == 1 and (t + 1) % tiles == 0:
+                    done = slice(t + 1 - tiles, t + 1)
+                    nc.sync.dma_start(out=piece_rows[:, done, :], in_=rows[:, done, :])
 
-        regroup(V, "g", 0, 0)
-        regroup(S, "g", 0, 1)
-        quantise("g", 0, 0)
         regroup(V, "x", 0, 0)
         regroup(S, "x", 1, 0)
-        quantise("g", 0, 1)
         quantise("x", 0, 0)
-        multiply_piece(0, 0, 0)
+        regroup(V, "g", 0, 0)
+        regroup(S, "g", 1, 0)
+        quantise("x", 1, 0)
+        quantise("g", 0, 0)
+        for n in (0, 1):
+            multiply_piece(0, n, 0)
         regroup(V, "x", 0, 1)
         regroup(S, "x", 1, 1)
-        quantise("x", 1, 0)
-        multiply_piece(0, 1, 0)
         quantise("x", 0, 1)
+        regroup(V, "g", 0, 1)
+        quantise("g", 0, 1)
         multiply_piece(0, 0, 1)
-        regroup(V, "g", 1, 0)
         quantise("x", 1, 1)
         multiply_piece(0, 1, 1)
-        empty_quarter(0, 0, False)
+        empty_quarter(0, 0, False, 2)
 
         regroup(V, "g", 1, 1)
         quantise("g", 1, 0)
         quantise("g", 1, 1)
         multiply_quarter(1, 0)
-        empty_quarter(1, 0, True)
+        empty_quarter(1, 0, True, 1)
 
         for n in (2, 3):
             regroup(V, "x", n, 0)
@@ -164,15 +162,20 @@ def tile_linearmem_kernel(tc, x, weight, bias, grad_out, out):
             multiply_piece(0, n, 0)
             quantise("x", n, 1)
             multiply_piece(0, n, 1)
-        empty_quarter(0, 1, False)
+        empty_quarter(0, 1, False, 1)
         multiply_quarter(1, 1)
-        empty_quarter(1, 1, True)
+        empty_quarter(1, 1, True, 1)
 
         for piece in (2, 3):
             regroup(V, "g", piece, 0)
             regroup(V, "g", piece, 1)
             quantise("g", piece, 0)
             quantise("g", piece, 1)
+
+        def store_tiles(m, count, rows):
+            first = m % M_PER_PIECE
+            piece_rows = out[(m - first) * M_TILE : (m - first + M_PER_PIECE) * M_TILE, :].rearrange("(p t) d -> p t d", p=P)
+            nc.sync.dma_start(out=piece_rows[:, first : first + count, :], in_=rows)
 
         for pair in range(M_TILES // 4, M_TILES // 2):
             rows = result.tile([P, 2, DIN], F32, name="rows")
@@ -182,7 +185,8 @@ def tile_linearmem_kernel(tc, x, weight, bias, grad_out, out):
                     for n in range(N_TILES):
                         multiply(m, n, c)
                 for n in range(N_TILES):
-                    copy = V if n % 2 == 1 and pair > M_TILES // 4 else S
-                    copy(out=rows[:, t, n * N_TILE : (n + 1) * N_TILE], in_=banks[m, n][:])
-            piece_rows = out[pair // 2 * PIECE : (pair // 2 + 1) * PIECE, :].rearrange("(p t) d -> p t d", p=P)
-            nc.sync.dma_start(out=piece_rows[:, pair % 2 * 2 : pair % 2 * 2 + 2, :], in_=rows[:])
+                    S(out=rows[:, t, n * N_TILE : (n + 1) * N_TILE], in_=banks[m, n][:])
+                if pair == M_TILES // 2 - 1:
+                    store_tiles(m, 1, rows[:, t : t + 1, :])
+            if pair < M_TILES // 2 - 1:
+                store_tiles(2 * pair, 2, rows[:])

@@ -49,13 +49,13 @@ def tile_linearmem_kernel(tc, x, weight, bias, grad_out, out):
                 at = piece * PIECE - first
                 raw_pieces[which, piece, c] = tile[:, :, at : at + PIECE]
 
-        for c in range(PASSES):
-            load("x", x_rows, c, 0, HALF)
-            load("g", g_rows, c, 0, HALF)
-        for c in range(PASSES):
-            load("x", x_rows, c, HALF, HALF)
-        for c in range(PASSES):
-            load("g", g_rows, c, HALF, HALF)
+        load("x", x_rows, 0, 0, HALF)
+        load("g", g_rows, 0, 0, HALF)
+        load("x", x_rows, 1, 0, HALF)
+        load("g", g_rows, 1, 0, DOUT)
+        load("x", x_rows, 0, HALF, HALF)
+        load("x", x_rows, 1, HALF, HALF)
+        load("g", g_rows, 0, HALF, HALF)
 
         codes = {
             "x": keep.tile([P, PASSES, DIN], U32, align_bytes=64, name="x_codes"),
@@ -68,23 +68,24 @@ def tile_linearmem_kernel(tc, x, weight, bias, grad_out, out):
         packed = {"x": E4M3_X4, "g": E5M2_X4}
         grouped_pieces = {}
 
-        def regroup(copy, which, piece, c):
-            grouped = stage.tile([P, PIECE, PACK], BF16, align_bytes=64, name="grouped")
-            order = "p (t m) j -> p m j t" if which == "g" else "p (m t) j -> p m j t"
+        def regroup(copy, which, piece, c, part=slice(0, PIECE)):
+            width = part.stop - part.start
+            grouped = stage.tile([P, width, PACK], BF16, align_bytes=64, name="grouped")
             copy(
-                out=grouped[:].rearrange(order, t=4),
-                in_=raw_pieces[which, piece, c].rearrange("p j (m t) -> p m j t", t=4),
+                out=grouped[:].rearrange("p (v i) j -> p v j i", i=4),
+                in_=raw_pieces[which, piece, c][:, :, part].rearrange("p j (v i) -> p v j i", i=4),
             )
-            grouped_pieces[which, piece, c] = grouped
+            grouped_pieces[which, piece, c, part.start] = grouped
 
-        def quantise(which, piece, c):
-            cols = slice(piece * PIECE, (piece + 1) * PIECE)
+        def quantise(which, piece, c, part=slice(0, PIECE)):
+            cols = slice(piece * PIECE + part.start, piece * PIECE + part.stop)
             nc.vector.quantize_mx(
                 out=codes[which][:, c, cols].bitcast(packed[which]),
                 scales=scales[which][:, c, cols],
-                in_=grouped_pieces[which, piece, c][:].rearrange("p v j -> p (v j)"),
+                in_=grouped_pieces[which, piece, c, part.start][:].rearrange("p v j -> p (v j)"),
             )
 
+        parts = (slice(0, PIECE // 2), slice(PIECE // 2, PIECE))
         banks = {}
 
         def multiply(m, n, c):
@@ -117,7 +118,7 @@ def tile_linearmem_kernel(tc, x, weight, bias, grad_out, out):
         def empty_quarter(g_piece, half, by_rows, stores):
             rows = result.tile([P, M_PER_PIECE, HALF], F32, name="rows")
             piece_rows = out[g_piece * PIECE : (g_piece + 1) * PIECE, half * HALF : (half + 1) * HALF].rearrange(
-                "(p t) d -> p t d", p=P
+                "(t p) d -> p t d", p=P
             )
             by_columns = [(t, n) for n in range(2) for t in range(M_PER_PIECE)]
             tiles = M_PER_PIECE // stores
@@ -137,56 +138,57 @@ def tile_linearmem_kernel(tc, x, weight, bias, grad_out, out):
         regroup(S, "g", 1, 0)
         quantise("x", 1, 0)
         quantise("g", 0, 0)
-        for n in (0, 1):
-            multiply_piece(0, n, 0)
+        multiply_piece(0, 0, 0)
+        multiply_piece(0, 1, 0)
         regroup(V, "x", 0, 1)
         regroup(S, "x", 1, 1)
-        quantise("x", 0, 1)
-        regroup(V, "g", 0, 1)
-        quantise("g", 0, 1)
-        multiply_piece(0, 0, 1)
-        quantise("x", 1, 1)
-        multiply_piece(0, 1, 1)
-        empty_quarter(0, 0, False, 2)
-
-        regroup(V, "g", 1, 1)
         quantise("g", 1, 0)
+        quantise("x", 0, 1)
+        quantise("x", 1, 1)
+        regroup(V, "g", 0, 1, parts[0])
+        quantise("g", 0, 1, parts[0])
+        for m in range(0, 2):
+            for n in (0, 1):
+                multiply(m, n, 1)
+        regroup(V, "g", 0, 1, parts[1])
+        regroup(V, "g", 1, 1)
+        quantise("g", 0, 1, parts[1])
+        for m in range(2, 4):
+            for n in (0, 1):
+                multiply(m, n, 1)
         quantise("g", 1, 1)
+        empty_quarter(0, 0, True, 2)
         multiply_quarter(1, 0)
-        empty_quarter(1, 0, True, 1)
-
-        for n in (2, 3):
-            regroup(V, "x", n, 0)
-            regroup(V, "x", n, 1)
-            quantise("x", n, 0)
-            multiply_piece(0, n, 0)
-            quantise("x", n, 1)
-            multiply_piece(0, n, 1)
-        empty_quarter(0, 1, False, 1)
+        empty_quarter(1, 0, True, 2)
+        regroup(V, "x", 2, 0)
+        regroup(V, "x", 2, 1)
+        quantise("x", 2, 0)
+        multiply_piece(0, 2, 0)
+        quantise("x", 2, 1)
+        multiply_piece(0, 2, 1)
+        regroup(V, "x", 3, 0)
+        regroup(V, "x", 3, 1)
+        quantise("x", 3, 0)
+        multiply_piece(0, 3, 0)
+        quantise("x", 3, 1)
+        multiply_piece(0, 3, 1)
+        empty_quarter(0, 1, False, 2)
         multiply_quarter(1, 1)
-        empty_quarter(1, 1, True, 1)
+        empty_quarter(1, 1, True, 2)
+        regroup(V, "g", 2, 0)
+        regroup(V, "g", 2, 1)
+        quantise("g", 2, 0)
+        quantise("g", 2, 1)
+        regroup(V, "g", 3, 0)
+        regroup(V, "g", 3, 1)
+        quantise("g", 3, 0)
+        quantise("g", 3, 1)
 
-        for piece in (2, 3):
-            regroup(V, "g", piece, 0)
-            regroup(V, "g", piece, 1)
-            quantise("g", piece, 0)
-            quantise("g", piece, 1)
-
-        def store_tiles(m, count, rows):
-            first = m % M_PER_PIECE
-            piece_rows = out[(m - first) * M_TILE : (m - first + M_PER_PIECE) * M_TILE, :].rearrange("(p t) d -> p t d", p=P)
-            nc.sync.dma_start(out=piece_rows[:, first : first + count, :], in_=rows)
-
-        for pair in range(M_TILES // 4, M_TILES // 2):
-            rows = result.tile([P, 2, DIN], F32, name="rows")
-            for t in range(2):
-                m = 2 * pair + t
-                for c in range(PASSES):
-                    for n in range(N_TILES):
-                        multiply(m, n, c)
+        for m in range(M_TILES // 2, M_TILES):
+            rows = result.tile([P, DIN], F32, name="rows")
+            for c in range(PASSES):
                 for n in range(N_TILES):
-                    S(out=rows[:, t, n * N_TILE : (n + 1) * N_TILE], in_=banks[m, n][:])
-                if pair == M_TILES // 2 - 1:
-                    store_tiles(m, 1, rows[:, t : t + 1, :])
-            if pair < M_TILES // 2 - 1:
-                store_tiles(2 * pair, 2, rows[:])
+                    multiply(m, n, c)
+            for n in range(N_TILES):
+                S(out=rows[:, n * N_TILE : (n + 1) * N_TILE], in_=banks[m, n][:])
+            nc.sync.dma_start(out=out[m * M_TILE : (m + 1) * M_TILE, :], in_=rows[:])

@@ -163,15 +163,17 @@ def tile_linearmem_kernel(tc, x, weight, bias, grad_out, out):
         regroup(V, "x", 2, 0)
         regroup(V, "x", 2, 1)
         quantise("x", 2, 0)
-        multiply_piece(0, 2, 0)
         quantise("x", 2, 1)
-        multiply_piece(0, 2, 1)
+        for m in range(0, 4):
+            for c in range(PASSES):
+                multiply(m, 2, c)
         regroup(V, "x", 3, 0)
         regroup(V, "x", 3, 1)
         quantise("x", 3, 0)
-        multiply_piece(0, 3, 0)
         quantise("x", 3, 1)
-        multiply_piece(0, 3, 1)
+        for m in range(0, 4):
+            for c in range(PASSES):
+                multiply(m, 3, c)
         empty_quarter(0, 1, False, 2)
         multiply_quarter(1, 1)
         empty_quarter(1, 1, True, 2)

from contextlib import ExitStack

import concourse.mybir as mybir

BF16 = mybir.dt.bfloat16
F32 = mybir.dt.float32
U32 = mybir.dt.uint32
U8 = mybir.dt.uint8
E4M3_X4 = mybir.dt.float8_e4m3fn_x4
E5M2_X4 = mybir.dt.float8_e5m2_x4

P = 128
PACK = 4
PASSES = 2
DIN = 2048
DOUT = 2048
M_TILE = 128
N_TILE = 512
M_TILES = DOUT // M_TILE
N_TILES = DIN // N_TILE
PSUM_BANKS = 8
PIECE = 512
M_PER_PIECE = PIECE // M_TILE
HALF = DIN // 2

FLOPS = 2 * PASSES * P * PACK * DIN * DOUT
BYTES = 2 * PASSES * P * PACK * (DIN + DOUT) + 4 * DIN * DOUT


def tile_linearmem_kernel(tc, x, weight, bias, grad_out, out):
    nc = tc.nc
    x_rows = x.rearrange("b (p j) d -> b p j d", j=PACK)
    g_rows = grad_out.rearrange("b (p j) e -> b p j e", j=PACK)

    with ExitStack() as ctx:
        raw = ctx.enter_context(tc.tile_pool(name="raw", bufs=1))
        keep = ctx.enter_context(tc.tile_pool(name="keep", bufs=1))
        stage = ctx.enter_context(tc.tile_pool(name="stage", bufs=6))
        result = ctx.enter_context(tc.tile_pool(name="result", bufs=6))
        psum = ctx.enter_context(tc.psum_pool(name="psum", bufs=PSUM_BANKS))
        ctx.enter_context(tc.manual_schedule())

        raw_pieces = {}

        def load(which, rows, c, first, width):
            tile = raw.tile([P, PACK, width], BF16, name="raw_%s%d_%d" % (which, c, first))
            nc.sync.dma_start(out=tile[:], in_=rows[c][:, :, first : first + width])
            for piece in range(first // PIECE, (first + width) // PIECE):
                at = piece * PIECE - first
                raw_pieces[which, piece, c] = tile[:, :, at : at + PIECE]

        load("x", x_rows, 0, 0, HALF)
        load("g", g_rows, 0, 0, HALF)
        load("x", x_rows, 1, 0, HALF)
        load("g", g_rows, 1, 0, DOUT)
        load("x", x_rows, 0, HALF, HALF)
        load("x", x_rows, 1, HALF, HALF)
        load("g", g_rows, 0, HALF, HALF)

        codes = {
            "x": keep.tile([P, PASSES, DIN], U32, align_bytes=64, name="x_codes"),
            "g": keep.tile([P, PASSES, DOUT], U32, align_bytes=64, name="g_codes"),
        }
        scales = {
            "x": keep.tile([P, PASSES, DIN], U8, align_bytes=64, name="x_scales"),
            "g": keep.tile([P, PASSES, DOUT], U8, align_bytes=64, name="g_scales"),
        }
        packed = {"x": E4M3_X4, "g": E5M2_X4}
        grouped_pieces = {}

        def regroup(copy, which, piece, c, part=slice(0, PIECE)):
            width = part.stop - part.start
            grouped = stage.tile([P, width, PACK], BF16, align_bytes=64, name="grouped")
            copy(
                out=grouped[:].rearrange("p (v i) j -> p v j i", i=4),
                in_=raw_pieces[which, piece, c][:, :, part].rearrange("p j (v i) -> p v j i", i=4),
            )
            grouped_pieces[which, piece, c, part.start] = grouped

        def quantise(which, piece, c, part=slice(0, PIECE)):
            cols = slice(piece * PIECE + part.start, piece * PIECE + part.stop)
            nc.vector.quantize_mx(
                out=codes[which][:, c, cols].bitcast(packed[which]),
                scales=scales[which][:, c, cols],
                in_=grouped_pieces[which, piece, c, part.start][:].rearrange("p v j -> p (v j)"),
            )

        parts = (slice(0, PIECE // 2), slice(PIECE // 2, PIECE))
        banks = {}

        def multiply(m, n, c):
            if c == 0:
                banks[m, n] = psum.tile([P, N_TILE], F32, name="bank")
            m_cols = slice(m * M_TILE, (m + 1) * M_TILE)
            n_cols = slice(n * N_TILE, (n + 1) * N_TILE)
            nc.tensor.matmul_mx(
                out=banks[m, n][:],
                lhsT=codes["g"][:, c, m_cols].bitcast(E5M2_X4),
                lhsT_scale=scales["g"][:, c, m_cols],
                rhs=codes["x"][:, c, n_cols].bitcast(E4M3_X4),
                rhs_scale=scales["x"][:, c, n_cols],
                start=(c == 0),
                stop=(c == PASSES - 1),
            )

        V, S = nc.vector.tensor_copy, nc.scalar.copy

        def multiply_piece(g_piece, n, c):
            for m in range(g_piece * M_PER_PIECE, (g_piece + 1) * M_PER_PIECE):
                multiply(m, n, c)

        def multiply_quarter(g_piece, half):
            for m in range(g_piece * M_PER_PIECE, (g_piece + 1) * M_PER_PIECE):
                for c in range(PASSES):
                    for n in (2 * half, 2 * half + 1):
                        multiply(m, n, c)

        def empty_quarter(g_piece, half, by_rows, stores):
            rows = result.tile([P, M_PER_PIECE, HALF], F32, name="rows")
            piece_rows = out[g_piece * PIECE : (g_piece + 1) * PIECE, half * HALF : (half + 1) * HALF].rearrange(
                "(t p) d -> p t d", p=P
            )
            by_columns = [(t, n) for n in range(2) for t in range(M_PER_PIECE)]
            tiles = M_PER_PIECE // stores
            for t, n in sorted(by_columns) if by_rows else by_columns:
                S(
                    out=rows[:, t, n * N_TILE : (n + 1) * N_TILE],
                    in_=banks[g_piece * M_PER_PIECE + t, 2 * half + n][:],
                )
                if n == 1 and (t + 1) % tiles == 0:
                    done = slice(t + 1 - tiles, t + 1)
                    nc.sync.dma_start(out=piece_rows[:, done, :], in_=rows[:, done, :])

        regroup(V, "x", 0, 0)
        regroup(S, "x", 1, 0)
        quantise("x", 0, 0)
        regroup(V, "g", 0, 0)
        regroup(S, "g", 1, 0)
        quantise("x", 1, 0)
        quantise("g", 0, 0)
        multiply_piece(0, 0, 0)
        multiply_piece(0, 1, 0)
        regroup(V, "x", 0, 1)
        regroup(S, "x", 1, 1)
        quantise("g", 1, 0)
        quantise("x", 0, 1)
        quantise("x", 1, 1)
        regroup(V, "g", 0, 1, parts[0])
        quantise("g", 0, 1, parts[0])
        for m in range(0, 2):
            for n in (0, 1):
                multiply(m, n, 1)
        regroup(V, "g", 0, 1, parts[1])
        regroup(V, "g", 1, 1)
        quantise("g", 0, 1, parts[1])
        for m in range(2, 4):
            for n in (0, 1):
                multiply(m, n, 1)
        quantise("g", 1, 1)
        empty_quarter(0, 0, True, 2)
        multiply_quarter(1, 0)
        empty_quarter(1, 0, True, 2)
        regroup(V, "x", 2, 0)
        regroup(V, "x", 2, 1)
        quantise("x", 2, 0)
        quantise("x", 2, 1)
        for m in range(0, 4):
            for c in range(PASSES):
                multiply(m, 2, c)
        regroup(V, "x", 3, 0)
        regroup(V, "x", 3, 1)
        quantise("x", 3, 0)
        quantise("x", 3, 1)
        for m in range(0, 4):
            for c in range(PASSES):
                multiply(m, 3, c)
        empty_quarter(0, 1, False, 2)
        multiply_quarter(1, 1)
        empty_quarter(1, 1, True, 2)
        regroup(V, "g", 2, 0)
        regroup(V, "g", 2, 1)
        quantise("g", 2, 0)
        quantise("g", 2, 1)
        regroup(V, "g", 3, 0)
        regroup(V, "g", 3, 1)
        quantise("g", 3, 0)
        quantise("g", 3, 1)

        for m in range(M_TILES // 2, M_TILES):
            rows = result.tile([P, DIN], F32, name="rows")
            for c in range(PASSES):
                for n in range(N_TILES):
                    multiply(m, n, c)
            for n in range(N_TILES):
                S(out=rows[:, n * N_TILE : (n + 1) * N_TILE], in_=banks[m, n][:])
            nc.sync.dma_start(out=out[m * M_TILE : (m + 1) * M_TILE, :], in_=rows[:])
